import numpy as np
import ml_dtypes


def mxq(x, axis, fmt="e4m3"):
    dtype, down = {"e4m3": (ml_dtypes.float8_e4m3fn, 7), "e5m2": (ml_dtypes.float8_e5m2, 14)}[fmt]
    v = np.moveaxis(np.asarray(x, np.float32).astype(ml_dtypes.bfloat16).astype(np.float64), axis, -1)
    blocks = v.reshape(v.shape[:-1] + (-1, 32))
    amax = np.abs(blocks).max(-1, keepdims=True)
    byte = np.maximum(np.where(amax > 0, np.frexp(amax)[1] - 1 + 127, 0) - down, 1)
    scale = np.exp2(byte - 127.0)
    codes = (blocks / scale).astype(np.float32).astype(dtype).astype(np.float64)
    return np.moveaxis((codes * scale).reshape(v.shape), -1, axis)


WIDE = False


def mx_kscale(k):
    if not WIDE:
        return np.ones(k)
    levels = np.array([10, -10, 5, -5, 0])
    a = np.random.permutation(np.resize(levels, k // 512 * 4)).reshape(k // 512, 4)
    idx = np.arange(k)
    return np.exp2(a[idx // 512, idx % 128 // 32])


BF16 = ml_dtypes.bfloat16


def bf(x):
    return np.asarray(x, np.float32).astype(BF16)


def f64(x):
    return np.asarray(x).astype(np.float64)


E2M1 = np.array([0.0, 0.5, 1.0, 1.5, 2.0, 3.0, 4.0, 6.0, -0.0, -0.5, -1.0, -1.5, -2.0, -3.0, -4.0, -6.0])


def pack_weight(w, fmt):
    k, n = w.shape
    w = f64(bf(w)).reshape(k // 32, 32, n)
    amax = np.abs(w).max(1)
    if fmt == "e4m3":
        byte = np.frexp(amax)[1] - 1 + 127 - 7
    else:
        mant, ex = np.frexp(amax / 6.0)
        byte = np.where(mant > 0.5, ex, ex - 1) + 127
    byte = np.clip(np.where(amax > 0, byte, 1), 1, 254)
    scaled = (w * np.exp2(127.0 - byte)[:, None, :]).reshape(k, n).astype(np.float32)
    by_word = np.ascontiguousarray(scaled.reshape(k // 512, 128, 4, n).transpose(0, 1, 3, 2))
    if fmt == "e4m3":
        words = by_word.astype(ml_dtypes.float8_e4m3fn).view(np.uint8)
    else:
        c = by_word.astype(ml_dtypes.float4_e2m1fn).view(np.uint8) & 0xF
        words = c[..., 0::2] | (c[..., 1::2] << 4)
    return np.ascontiguousarray(words), np.ascontiguousarray(byte.astype(np.uint8).reshape(k // 512, 16, n))


def unpack_weight(words, scales, fmt):
    g, p, n, _ = words.shape
    if fmt == "e4m3":
        vals = np.ascontiguousarray(words).view(ml_dtypes.float8_e4m3fn).astype(np.float64)
    else:
        nib = np.empty((g, p, n, 4), np.uint8)
        nib[..., 0::2] = words & 0xF
        nib[..., 1::2] = words >> 4
        vals = E2M1[nib]
    vals = vals * np.repeat(np.exp2(scales.astype(np.float64) - 127.0), 8, axis=1)[..., None]
    return vals.transpose(0, 1, 3, 2).reshape(g * 512, n)

def pack4(w):
    words, scales = pack_weight(w, "e2m1")
    return words.reshape(words.shape[0], 128, -1), scales


def unpack4(words, scales):
    return unpack_weight(words.reshape(words.shape[0], 128, -1, 2), scales, "e2m1")


N, K, H, A = 2048, 2, 256, 10
D = K * H
T = A * H


def sigmoid(v):
    return 1.0 / (1.0 + np.exp(-v))


def setup_inputs():
    s = mx_kscale(D)
    h_mail = np.random.standard_normal((N, K, H)) * s.reshape(K, H)
    c_mail = np.random.standard_normal((N, K, H))
    U_f_w = np.random.standard_normal((T, T)) / np.sqrt(D)
    U_f_w[:D] = U_f_w[:D] / s[:, None]
    U_f_b = np.random.standard_normal(T) * 0.5
    U_iou_w = np.random.standard_normal((3 * H, T)) / np.sqrt(D)
    U_iou_w[:, :D] = U_iou_w[:, :D] / s
    b_iou = np.random.standard_normal((1, 3 * H)) * 0.3
    U_f_w_words, U_f_w_scales = pack4(U_f_w)
    U_iou_w_words, U_iou_w_scales = pack4(np.ascontiguousarray(U_iou_w.T))
    return {"h_mail": bf(h_mail), "c_mail": bf(c_mail), "U_f_w_words": U_f_w_words, "U_f_w_scales": U_f_w_scales, "U_f_b": bf(U_f_b), "U_iou_w_words": U_iou_w_words, "U_iou_w_scales": U_iou_w_scales, "b_iou": bf(b_iou)}


def reference(h_mail, c_mail, U_f_w_words, U_f_w_scales, U_f_b, U_iou_w_words, U_iou_w_scales, b_iou):
    n, k, h = h_mail.shape
    d = k * h
    hq = mxq(f64(h_mail).reshape(n, d), 1, "e4m3")
    f = sigmoid((hq @ unpack4(U_f_w_words, U_f_w_scales)[:d, :d]) + f64(U_f_b)[:d])
    c_red = np.sum(f.reshape(n, k, h) * f64(c_mail), axis=1)
    iou = (hq @ unpack4(U_iou_w_words, U_iou_w_scales)[:d, :]) + f64(b_iou)
    i, o, u = np.split(iou, 3, axis=1)
    c = sigmoid(i) * np.tanh(u) + c_red
    h_out = sigmoid(o) * np.tanh(c)
    return h_out, c

@@ -1,0 +1,251 @@
+from contextlib import ExitStack
+
+import concourse.mybir as mybir
+from concourse.masks import make_identity
+
+F32 = mybir.dt.float32
+BF16 = mybir.dt.bfloat16
+I32 = mybir.dt.int32
+U32 = mybir.dt.uint32
+U8 = mybir.dt.uint8
+FP8X4 = mybir.dt.float8_e4m3fn_x4
+FP4X4 = mybir.dt.float4_e2m1fn_x4
+ACT = mybir.ActivationFunctionType
+ALU = mybir.AluOpType
+
+P = 128
+NODES = 2048
+CHILDREN = 2
+HID = 256
+D = CHILDREN * HID
+TILES = NODES // P
+CHUNK_TILES = 4
+CHUNKS = TILES // CHUNK_TILES
+CHUNK = CHUNK_TILES * P
+HALVES = HID // P
+F_COLS = D
+IOU_COLS = 3 * HID
+W_COLS = F_COLS + IOU_COLS
+GATE_TILES = W_COLS // P
+
+FLOPS = 2 * NODES * D * W_COLS
+BYTES = (
+    2 * NODES * D * 2
+    + P * W_COLS * 2 + 16 * W_COLS
+    + W_COLS * 2
+    + 2 * NODES * HID * 4
+)
+
+
+UNITS = CHUNKS * HALVES
+PAIRS = TILES // 2
+
+
+def tile_treelstmcell_kernel(
+    tc, h_mail, c_mail, U_f_w_words, U_f_w_scales, U_f_b, U_iou_w_words, U_iou_w_scales, b_iou, out_0, out_1
+):
+    nc = tc.nc
+    h_view = h_mail.rearrange("(p t) k j -> p t (k j)", t=TILES)
+    cm_view = c_mail.rearrange("(p t) k j -> p t (k j)", t=TILES)
+    h_out_view = out_0.rearrange("(p t) j -> p t j", t=TILES)
+    c_out_view = out_1.rearrange("(p t) j -> p t j", t=TILES)
+
+    with ExitStack() as ctx:
+        ctx.enter_context(tc.manual_schedule())
+        keep = ctx.enter_context(tc.tile_pool(name="keep", bufs=1))
+        loads = ctx.enter_context(tc.tile_pool(name="loads", bufs=CHUNKS))
+        work = ctx.enter_context(tc.tile_pool(name="work", bufs=4))
+        psum = ctx.enter_context(tc.psum_pool(name="psum", bufs=1))
+
+        w_scales = keep.tile([P, W_COLS], U8, align_bytes=64)
+        nc.vector.memset(w_scales[:].bitcast(I32), 0)
+        bias_rows = keep.tile([P, P], BF16)
+        nc.vector.memset(bias_rows[:], 0.0)
+        warm = keep.tile([P, 1], F32)
+        nc.vector.memset(warm[:], 0.0)
+        nc.scalar.activation(out=warm[:], in_=warm[:], func=ACT.Sigmoid)
+
+        ident_f32 = keep.tile([P, P], F32)
+        make_identity(nc, ident_f32[:])
+        ident_bf16 = keep.tile([P, P], BF16)
+        make_identity(nc, ident_bf16[:])
+
+        h_sb = []
+        cm_sb = []
+        for c in range(CHUNKS):
+            h_sb.append(loads.tile([P, CHUNK_TILES, D], BF16, name="h_sb", tag="h_sb"))
+            cm_sb.append(loads.tile([P, CHUNK_TILES, D], BF16, name="cm_sb", tag="cm_sb"))
+        tiles_of = [slice(c * CHUNK_TILES, (c + 1) * CHUNK_TILES) for c in range(CHUNKS)]
+
+        nc.sync.dma_start(out=h_sb[0][:], in_=h_view[:, tiles_of[0], :])
+        w_words = keep.tile([P, 2 * W_COLS], U8, align_bytes=64)
+        for quad in range(4):
+            rows = slice(4 * quad, 4 * quad + 4)
+            parts = slice(32 * quad, 32 * quad + 4)
+            nc.sync.dma_start(
+                out=w_scales[parts, 0:F_COLS].bitcast(I32), in_=U_f_w_scales[0, rows, 0:F_COLS].bitcast(I32)
+            )
+        nc.sync.dma_start(out=w_words[:, 0 : 2 * F_COLS].bitcast(I32), in_=U_f_w_words[0, :, 0 : 2 * F_COLS].bitcast(I32))
+        nc.sync.dma_start(out=bias_rows[0 : F_COLS // P, :], in_=U_f_b[0:F_COLS].rearrange("(m p) -> m p", p=P))
+        nc.sync.dma_start(out=bias_rows[F_COLS // P : GATE_TILES, :], in_=b_iou[0, :].rearrange("(m p) -> m p", p=P))
+        for quad in range(4):
+            rows = slice(4 * quad, 4 * quad + 4)
+            parts = slice(32 * quad, 32 * quad + 4)
+            nc.sync.dma_start(
+                out=w_scales[parts, F_COLS:W_COLS].bitcast(I32), in_=U_iou_w_scales[0, rows, :].bitcast(I32)
+            )
+        nc.sync.dma_start(out=w_words[:, 2 * F_COLS : 2 * W_COLS].bitcast(I32), in_=U_iou_w_words[0, :, :].bitcast(I32))
+        nc.sync.dma_start(out=cm_sb[0][:], in_=cm_view[:, tiles_of[0], :])
+        for c in range(1, CHUNKS):
+            nc.sync.dma_start(out=h_sb[c][:], in_=h_view[:, tiles_of[c], :])
+            nc.sync.dma_start(out=cm_sb[c][:], in_=cm_view[:, tiles_of[c], :])
+
+        codes = [keep.tile([P, CHUNK], U32, align_bytes=64, name="codes%d" % c) for c in range(CHUNKS)]
+        scales = [keep.tile([P, CHUNK], U8, align_bytes=64, name="scales%d" % c) for c in range(CHUNKS)]
+        bias_sb = keep.tile([P, GATE_TILES], F32)
+        live = {}
+
+        def turn_h(g):
+            hT_ps = psum.tile([P, 2, 2, P], F32, tag="turn", bufs=3)
+            for a in range(2):
+                words = h_sb[g // 2][:, 2 * (g % 2) + a, :].bitcast(F32)
+                for u in range(2):
+                    nc.tensor.transpose(hT_ps[:, a, u, :], words[:, u : D // 2 : 2], ident_f32[:])
+            live["hT_ps", g] = hT_ps
+
+        def group_h(g):
+            grouped = work.tile([P, 2 * P, 4], BF16, align_bytes=64, tag="grouped")
+            flat = grouped[:].rearrange("p n t -> p (n t)")
+            nc.vector.tensor_copy(
+                out=flat.bitcast(F32).rearrange("p (a n u) -> p a n u", a=2, u=2),
+                in_=live["hT_ps", g][:].rearrange("p a u n -> p a n u"),
+            )
+            live["flat", g] = flat
+
+        def quantise_h(g):
+            cols = slice(2 * P * (g % 2), 2 * P * (g % 2 + 1))
+            nc.vector.quantize_mx(
+                out=codes[g // 2][:, cols].bitcast(FP8X4), scales=scales[g // 2][:, cols], in_=live["flat", g]
+            )
+
+        def turn_cm(q):
+            c, half = divmod(q, HALVES)
+            cm_ps = psum.tile([P, CHILDREN, CHUNK], BF16, tag="cm_ps")
+            for k in range(CHILDREN):
+                for t in range(CHUNK_TILES):
+                    nc.tensor.transpose(
+                        cm_ps[:, k, P * t : P * (t + 1)],
+                        cm_sb[c][:, t, HID * k + P * half : HID * k + P * (half + 1)],
+                        ident_bf16[:],
+                    )
+            live["cm_ps", q] = cm_ps
+
+        def gate_pass(q, m):
+            gate_ps = psum.tile([P, CHUNK], F32, tag="gate_ps", bufs=4)
+            nc.tensor.matmul_mx(
+                out=gate_ps[:],
+                lhsT=w_words[:, 2 * P * m : 2 * P * (m + 1)].bitcast(FP4X4),
+                lhsT_scale=w_scales[:, P * m : P * (m + 1)],
+                rhs=codes[q // HALVES][:].bitcast(FP8X4),
+                rhs_scale=scales[q // HALVES][:],
+                start=True,
+                stop=True,
+            )
+            return gate_ps
+
+        def gates(q):
+            half = q % HALVES
+            f_sb = work.tile([P, CHILDREN, CHUNK], F32, tag="f_sb")
+            i_sb = work.tile([P, CHUNK], F32, tag="i_sb")
+            o_sb = work.tile([P, CHUNK], F32, tag="o_sb")
+            u_sb = work.tile([P, CHUNK], F32, tag="u_sb")
+            plan = [
+                (0 + half, ACT.Sigmoid, f_sb[:, 0, :]),
+                (2 + half, ACT.Sigmoid, f_sb[:, 1, :]),
+                (4 + half, ACT.Sigmoid, i_sb[:]),
+                (8 + half, ACT.Tanh, u_sb[:]),
+                (6 + half, ACT.Sigmoid, o_sb[:]),
+            ]
+            banks = [gate_pass(q, m) for m, func, dest in plan]
+            for (m, func, dest), gate_ps in zip(plan, banks):
+                nc.scalar.activation(out=dest, in_=gate_ps[:], func=func, bias=bias_sb[:, m : m + 1], scale=1.0)
+            live["f_sb", q], live["i_sb", q], live["o_sb", q], live["u_sb", q] = f_sb, i_sb, o_sb, u_sb
+
+        def products(q):
+            prod = work.tile([P, CHILDREN, CHUNK], F32, tag="prod")
+            nc.vector.tensor_tensor(out=prod[:], in0=live["f_sb", q][:], in1=live["cm_ps", q][:], op=ALU.mult)
+            c_red = work.tile([P, CHUNK], F32, tag="c_red")
+            nc.gpsimd.tensor_tensor(out=c_red[:], in0=prod[:, 0, :], in1=prod[:, 1, :], op=ALU.add)
+            iu = work.tile([P, CHUNK], F32, tag="iu")
+            nc.gpsimd.tensor_tensor(out=iu[:], in0=live["i_sb", q][:], in1=live["u_sb", q][:], op=ALU.mult)
+            live["c_red", q], live["iu", q] = c_red, iu
+
+        def cell(q):
+            cT = work.tile([P, CHUNK], F32, tag="cT")
+            nc.vector.tensor_tensor(out=cT[:], in0=live["iu", q][:], in1=live["c_red", q][:], op=ALU.add)
+            live["cT", q] = cT
+
+        def turn_back(q):
+            c_ps = psum.tile([P, CHUNK_TILES, P], F32, tag="turn", bufs=3)
+            o_ps = psum.tile([P, CHUNK_TILES, P], F32, tag="turn", bufs=3)
+            for t in range(CHUNK_TILES):
+                nc.tensor.transpose(c_ps[:, t, :], live["cT", q][:, P * t : P * (t + 1)], ident_f32[:])
+            for t in range(CHUNK_TILES):
+                nc.tensor.transpose(o_ps[:, t, :], live["o_sb", q][:, P * t : P * (t + 1)], ident_f32[:])
+            live["c_ps", q], live["o_ps", q] = c_ps, o_ps
+
+        def cell_out(q):
+            c, half = divmod(q, HALVES)
+            feats = slice(P * half, P * (half + 1))
+            if half == 0:
+                live["c_out", c] = work.tile([P, CHUNK_TILES, HID], F32, name="c_out", tag="c_out")
+                live["h_out", c] = work.tile([P, CHUNK_TILES, HID], F32, name="h_out", tag="h_out")
+            nc.vector.tensor_copy(out=live["c_out", c][:, :, feats], in_=live["c_ps", q][:])
+            tanh_c = work.tile([P, CHUNK_TILES, P], F32, tag="tanh_c")
+            nc.scalar.activation(out=tanh_c[:], in_=live["c_out", c][:, :, feats], func=ACT.Tanh)
+            live["tanh_c", q] = tanh_c
+            if half == HALVES - 1:
+                nc.sync.dma_start(out=c_out_view[:, tiles_of[c], :], in_=live["c_out", c][:])
+
+        def hidden_out(q):
+            c, half = divmod(q, HALVES)
+            feats = slice(P * half, P * (half + 1))
+            nc.vector.tensor_tensor(
+                out=live["h_out", c][:, :, feats], in0=live["tanh_c", q][:], in1=live["o_ps", q][:], op=ALU.mult
+            )
+            if half == HALVES - 1:
+                nc.sync.dma_start(out=h_out_view[:, tiles_of[c], :], in_=live["h_out", c][:])
+
+        turn_h(0)
+        turn_h(1)
+        group_h(0)
+        group_h(1)
+        quantise_h(0)
+        bias_ps = psum.tile([P, CHILDREN, CHUNK], BF16, tag="cm_ps")
+        nc.tensor.transpose(bias_ps[:, 0, 0:P], bias_rows[:], ident_bf16[:])
+        nc.vector.tensor_copy(out=bias_sb[:], in_=bias_ps[:, 0, 0:GATE_TILES])
+        quantise_h(1)
+
+        for q in range(UNITS + 3):
+            if q < UNITS:
+                gates(q)
+                turn_cm(q)
+            if 0 <= q - 3 < UNITS:
+                hidden_out(q - 3)
+            if q == 1:
+                quantise_h(2)
+            if 1 <= q and q + 2 < PAIRS:
+                quantise_h(q + 2)
+            if q < UNITS:
+                products(q)
+            if 0 <= q - 2 < UNITS:
+                turn_back(q - 2)
+                cell_out(q - 2)
+            if 0 <= q - 1 < UNITS:
+                cell(q - 1)
+            if q == 0:
+                turn_h(2)
+                group_h(2)
+            if q + 3 < PAIRS:
+                turn_h(q + 3)
+                group_h(q + 3)

@@ -19,10 +19,13 @@ CHILDREN = 2
 HID = 256
 D = CHILDREN * HID
 TILES = NODES // P
-CHUNK_TILES = 4
-CHUNKS = TILES // CHUNK_TILES
-CHUNK = CHUNK_TILES * P
+PAIRS = TILES // 2
+PAIR = 2 * P
+CHUNK_PAIRS = (2, 2, 2, 1, 1)
+CHUNKS = len(CHUNK_PAIRS)
+WIDEST = max(CHUNK_PAIRS) * PAIR
 HALVES = HID // P
+UNITS = CHUNKS * HALVES
 F_COLS = D
 IOU_COLS = 3 * HID
 W_COLS = F_COLS + IOU_COLS
@@ -37,10 +40,6 @@ BYTES = (
 )
 
 
-UNITS = CHUNKS * HALVES
-PAIRS = TILES // 2
-
-
 def tile_treelstmcell_kernel(
     tc, h_mail, c_mail, U_f_w_words, U_f_w_scales, U_f_b, U_iou_w_words, U_iou_w_scales, b_iou, out_0, out_1
 ):
@@ -50,71 +49,80 @@ def tile_treelstmcell_kernel(
     h_out_view = out_0.rearrange("(p t) j -> p t j", t=TILES)
     c_out_view = out_1.rearrange("(p t) j -> p t j", t=TILES)
 
+    first_pair = [sum(CHUNK_PAIRS[:c]) for c in range(CHUNKS)]
+    chunk_of_pair = [c for c in range(CHUNKS) for g in range(CHUNK_PAIRS[c])]
+    tiles_in = [2 * CHUNK_PAIRS[c] for c in range(CHUNKS)]
+    width = [PAIR * CHUNK_PAIRS[c] for c in range(CHUNKS)]
+    tiles_of = [slice(2 * first_pair[c], 2 * first_pair[c] + tiles_in[c]) for c in range(CHUNKS)]
+
     with ExitStack() as ctx:
         ctx.enter_context(tc.manual_schedule())
         keep = ctx.enter_context(tc.tile_pool(name="keep", bufs=1))
-        loads = ctx.enter_context(tc.tile_pool(name="loads", bufs=CHUNKS))
-        work = ctx.enter_context(tc.tile_pool(name="work", bufs=4))
+        work = ctx.enter_context(tc.tile_pool(name="work", bufs=5))
         psum = ctx.enter_context(tc.psum_pool(name="psum", bufs=1))
 
-        w_scales = keep.tile([P, W_COLS], U8, align_bytes=64)
-        nc.vector.memset(w_scales[:].bitcast(I32), 0)
+        cols_of = {"f": F_COLS, "iou": IOU_COLS}
+        bias_col = {"f": 0, "iou": F_COLS // P}
+        w_words = {}
+        w_scales = {}
+        for w in ("f", "iou"):
+            w_words[w] = keep.tile([P, 2 * cols_of[w]], U8, align_bytes=64, name="w_words_" + w)
+            w_scales[w] = keep.tile([P, cols_of[w]], U8, align_bytes=64, name="w_scales_" + w)
         bias_rows = keep.tile([P, P], BF16)
+        bias_sb = keep.tile([P, GATE_TILES], F32)
+        h_sb = [keep.tile([P, tiles_in[c], D], BF16, name="h_sb%d" % c) for c in range(CHUNKS)]
+        cm_sb = [keep.tile([P, tiles_in[c], D], BF16, name="cm_sb%d" % c) for c in range(CHUNKS)]
+        codes = [keep.tile([P, width[c]], U32, align_bytes=64, name="codes%d" % c) for c in range(CHUNKS)]
+        scales = [keep.tile([P, width[c]], U8, align_bytes=64, name="scales%d" % c) for c in range(CHUNKS)]
+
         nc.vector.memset(bias_rows[:], 0.0)
+        for w in ("f", "iou"):
+            nc.vector.memset(w_scales[w][:].bitcast(I32), 0)
+        nc.gpsimd.dma_start(out=bias_rows[0 : F_COLS // P, :], in_=U_f_b[0:F_COLS].rearrange("(m p) -> m p", p=P))
+        nc.gpsimd.dma_start(out=bias_rows[F_COLS // P : GATE_TILES, :], in_=b_iou[0, :].rearrange("(m p) -> m p", p=P))
+        nc.scalar.dma_start(out=h_sb[0][:], in_=h_view[:, tiles_of[0], :])
+
+        def load_weight(w, words, scale_rows):
+            for quad in range(4):
+                nc.sync.dma_start(
+                    out=w_scales[w][32 * quad : 32 * quad + 4, :].bitcast(I32),
+                    in_=scale_rows[4 * quad : 4 * quad + 4, :].bitcast(I32),
+                )
+            nc.sync.dma_start(out=w_words[w][:].bitcast(I32), in_=words.bitcast(I32))
+
+        load_weight("f", U_f_w_words[0, :, 0 : 2 * F_COLS], U_f_w_scales[0, :, 0:F_COLS])
+        load_weight("iou", U_iou_w_words[0, :, :], U_iou_w_scales[0, :, :])
+        for c in range(CHUNKS):
+            if c + 1 < CHUNKS:
+                nc.sync.dma_start(out=h_sb[c + 1][:], in_=h_view[:, tiles_of[c + 1], :])
+            nc.sync.dma_start(out=cm_sb[c][:], in_=cm_view[:, tiles_of[c], :])
+
         warm = keep.tile([P, 1], F32)
         nc.vector.memset(warm[:], 0.0)
         nc.scalar.activation(out=warm[:], in_=warm[:], func=ACT.Sigmoid)
-
         ident_f32 = keep.tile([P, P], F32)
         make_identity(nc, ident_f32[:])
         ident_bf16 = keep.tile([P, P], BF16)
-        make_identity(nc, ident_bf16[:])
+        nc.vector.tensor_copy(out=ident_bf16[:], in_=ident_f32[:])
 
-        h_sb = []
-        cm_sb = []
-        for c in range(CHUNKS):
-            h_sb.append(loads.tile([P, CHUNK_TILES, D], BF16, name="h_sb", tag="h_sb"))
-            cm_sb.append(loads.tile([P, CHUNK_TILES, D], BF16, name="cm_sb", tag="cm_sb"))
-        tiles_of = [slice(c * CHUNK_TILES, (c + 1) * CHUNK_TILES) for c in range(CHUNKS)]
-
-        nc.sync.dma_start(out=h_sb[0][:], in_=h_view[:, tiles_of[0], :])
-        w_words = keep.tile([P, 2 * W_COLS], U8, align_bytes=64)
-        for quad in range(4):
-            rows = slice(4 * quad, 4 * quad + 4)
-            parts = slice(32 * quad, 32 * quad + 4)
-            nc.sync.dma_start(
-                out=w_scales[parts, 0:F_COLS].bitcast(I32), in_=U_f_w_scales[0, rows, 0:F_COLS].bitcast(I32)
-            )
-        nc.sync.dma_start(out=w_words[:, 0 : 2 * F_COLS].bitcast(I32), in_=U_f_w_words[0, :, 0 : 2 * F_COLS].bitcast(I32))
-        nc.sync.dma_start(out=bias_rows[0 : F_COLS // P, :], in_=U_f_b[0:F_COLS].rearrange("(m p) -> m p", p=P))
-        nc.sync.dma_start(out=bias_rows[F_COLS // P : GATE_TILES, :], in_=b_iou[0, :].rearrange("(m p) -> m p", p=P))
-        for quad in range(4):
-            rows = slice(4 * quad, 4 * quad + 4)
-            parts = slice(32 * quad, 32 * quad + 4)
-            nc.sync.dma_start(
-                out=w_scales[parts, F_COLS:W_COLS].bitcast(I32), in_=U_iou_w_scales[0, rows, :].bitcast(I32)
-            )
-        nc.sync.dma_start(out=w_words[:, 2 * F_COLS : 2 * W_COLS].bitcast(I32), in_=U_iou_w_words[0, :, :].bitcast(I32))
-        nc.sync.dma_start(out=cm_sb[0][:], in_=cm_view[:, tiles_of[0], :])
-        for c in range(1, CHUNKS):
-            nc.sync.dma_start(out=h_sb[c][:], in_=h_view[:, tiles_of[c], :])
-            nc.sync.dma_start(out=cm_sb[c][:], in_=cm_view[:, tiles_of[c], :])
-
-        codes = [keep.tile([P, CHUNK], U32, align_bytes=64, name="codes%d" % c) for c in range(CHUNKS)]
-        scales = [keep.tile([P, CHUNK], U8, align_bytes=64, name="scales%d" % c) for c in range(CHUNKS)]
-        bias_sb = keep.tile([P, GATE_TILES], F32)
         live = {}
 
+        def turn_bias():
+            bias_ps = psum.tile([P, CHILDREN, WIDEST], BF16, tag="cm_ps")
+            nc.tensor.transpose(bias_ps[:, 0, 0:P], bias_rows[:], ident_bf16[:])
+            nc.vector.tensor_copy(out=bias_sb[:], in_=bias_ps[:, 0, 0:GATE_TILES])
+
         def turn_h(g):
+            c = chunk_of_pair[g]
             hT_ps = psum.tile([P, 2, 2, P], F32, tag="turn", bufs=3)
             for a in range(2):
-                words = h_sb[g // 2][:, 2 * (g % 2) + a, :].bitcast(F32)
+                words = h_sb[c][:, 2 * (g - first_pair[c]) + a, :].bitcast(F32)
                 for u in range(2):
                     nc.tensor.transpose(hT_ps[:, a, u, :], words[:, u : D // 2 : 2], ident_f32[:])
             live["hT_ps", g] = hT_ps
 
         def group_h(g):
-            grouped = work.tile([P, 2 * P, 4], BF16, align_bytes=64, tag="grouped")
+            grouped = work.tile([P, PAIR, 4], BF16, align_bytes=64, tag="grouped")
             flat = grouped[:].rearrange("p n t -> p (n t)")
             nc.vector.tensor_copy(
                 out=flat.bitcast(F32).rearrange("p (a n u) -> p a n u", a=2, u=2),
@@ -123,16 +131,15 @@ def tile_treelstmcell_kernel(
             live["flat", g] = flat
 
         def quantise_h(g):
-            cols = slice(2 * P * (g % 2), 2 * P * (g % 2 + 1))
-            nc.vector.quantize_mx(
-                out=codes[g // 2][:, cols].bitcast(FP8X4), scales=scales[g // 2][:, cols], in_=live["flat", g]
-            )
+            c = chunk_of_pair[g]
+            cols = slice(PAIR * (g - first_pair[c]), PAIR * (g - first_pair[c] + 1))
+            nc.vector.quantize_mx(out=codes[c][:, cols].bitcast(FP8X4), scales=scales[c][:, cols], in_=live["flat", g])
 
         def turn_cm(q):
             c, half = divmod(q, HALVES)
-            cm_ps = psum.tile([P, CHILDREN, CHUNK], BF16, tag="cm_ps")
+            cm_ps = psum.tile([P, CHILDREN, WIDEST], BF16, tag="cm_ps")
             for k in range(CHILDREN):
-                for t in range(CHUNK_TILES):
+                for t in range(tiles_in[c]):
                     nc.tensor.transpose(
                         cm_ps[:, k, P * t : P * (t + 1)],
                         cm_sb[c][:, t, HID * k + P * half : HID * k + P * (half + 1)],
@@ -140,112 +147,113 @@ def tile_treelstmcell_kernel(
                     )
             live["cm_ps", q] = cm_ps
 
-        def gate_pass(q, m):
-            gate_ps = psum.tile([P, CHUNK], F32, tag="gate_ps", bufs=4)
+        def gate_pass(c, w, m):
+            gate_ps = psum.tile([P, WIDEST], F32, tag="gate_ps", bufs=4)
             nc.tensor.matmul_mx(
-                out=gate_ps[:],
-                lhsT=w_words[:, 2 * P * m : 2 * P * (m + 1)].bitcast(FP4X4),
-                lhsT_scale=w_scales[:, P * m : P * (m + 1)],
-                rhs=codes[q // HALVES][:].bitcast(FP8X4),
-                rhs_scale=scales[q // HALVES][:],
+                out=gate_ps[:, 0 : width[c]],
+                lhsT=w_words[w][:, 2 * P * m : 2 * P * (m + 1)].bitcast(FP4X4),
+                lhsT_scale=w_scales[w][:, P * m : P * (m + 1)],
+                rhs=codes[c][:].bitcast(FP8X4),
+                rhs_scale=scales[c][:],
                 start=True,
                 stop=True,
             )
             return gate_ps
 
         def gates(q):
-            half = q % HALVES
-            f_sb = work.tile([P, CHILDREN, CHUNK], F32, tag="f_sb")
-            i_sb = work.tile([P, CHUNK], F32, tag="i_sb")
-            o_sb = work.tile([P, CHUNK], F32, tag="o_sb")
-            u_sb = work.tile([P, CHUNK], F32, tag="u_sb")
+            c, half = divmod(q, HALVES)
+            f_sb = work.tile([P, CHILDREN, width[c]], F32, tag="f_sb")
+            i_sb = work.tile([P, width[c]], F32, tag="i_sb")
+            o_sb = work.tile([P, width[c]], F32, tag="o_sb")
+            u_sb = work.tile([P, width[c]], F32, tag="u_sb")
             plan = [
-                (0 + half, ACT.Sigmoid, f_sb[:, 0, :]),
-                (2 + half, ACT.Sigmoid, f_sb[:, 1, :]),
-                (4 + half, ACT.Sigmoid, i_sb[:]),
-                (8 + half, ACT.Tanh, u_sb[:]),
-                (6 + half, ACT.Sigmoid, o_sb[:]),
+                ("f", 0 * HALVES + half, ACT.Sigmoid, f_sb[:, 0, :]),
+                ("f", 1 * HALVES + half, ACT.Sigmoid, f_sb[:, 1, :]),
+                ("iou", 0 * HALVES + half, ACT.Sigmoid, i_sb[:]),
+                ("iou", 2 * HALVES + half, ACT.Tanh, u_sb[:]),
+                ("iou", 1 * HALVES + half, ACT.Sigmoid, o_sb[:]),
             ]
-            banks = [gate_pass(q, m) for m, func, dest in plan]
-            for (m, func, dest), gate_ps in zip(plan, banks):
-                nc.scalar.activation(out=dest, in_=gate_ps[:], func=func, bias=bias_sb[:, m : m + 1], scale=1.0)
+            banks = [gate_pass(c, w, m) for w, m, func, dest in plan]
+            for (w, m, func, dest), gate_ps in zip(plan, banks):
+                col = bias_col[w] + m
+                nc.scalar.activation(
+                    out=dest, in_=gate_ps[:, 0 : width[c]], func=func, bias=bias_sb[:, col : col + 1], scale=1.0
+                )
             live["f_sb", q], live["i_sb", q], live["o_sb", q], live["u_sb", q] = f_sb, i_sb, o_sb, u_sb
 
         def products(q):
-            prod = work.tile([P, CHILDREN, CHUNK], F32, tag="prod")
-            nc.vector.tensor_tensor(out=prod[:], in0=live["f_sb", q][:], in1=live["cm_ps", q][:], op=ALU.mult)
-            c_red = work.tile([P, CHUNK], F32, tag="c_red")
+            c = q // HALVES
+            prod = work.tile([P, CHILDREN, width[c]], F32, tag="prod")
+            nc.vector.tensor_tensor(
+                out=prod[:], in0=live["f_sb", q][:], in1=live["cm_ps", q][:, :, 0 : width[c]], op=ALU.mult
+            )
+            c_red = work.tile([P, width[c]], F32, tag="c_red")
             nc.gpsimd.tensor_tensor(out=c_red[:], in0=prod[:, 0, :], in1=prod[:, 1, :], op=ALU.add)
-            iu = work.tile([P, CHUNK], F32, tag="iu")
+            iu = work.tile([P, width[c]], F32, tag="iu")
             nc.gpsimd.tensor_tensor(out=iu[:], in0=live["i_sb", q][:], in1=live["u_sb", q][:], op=ALU.mult)
             live["c_red", q], live["iu", q] = c_red, iu
-
-        def cell(q):
-            cT = work.tile([P, CHUNK], F32, tag="cT")
-            nc.vector.tensor_tensor(out=cT[:], in0=live["iu", q][:], in1=live["c_red", q][:], op=ALU.add)
-            live["cT", q] = cT
-
-        def turn_back(q):
-            c_ps = psum.tile([P, CHUNK_TILES, P], F32, tag="turn", bufs=3)
-            o_ps = psum.tile([P, CHUNK_TILES, P], F32, tag="turn", bufs=3)
-            for t in range(CHUNK_TILES):
-                nc.tensor.transpose(c_ps[:, t, :], live["cT", q][:, P * t : P * (t + 1)], ident_f32[:])
-            for t in range(CHUNK_TILES):
-                nc.tensor.transpose(o_ps[:, t, :], live["o_sb", q][:, P * t : P * (t + 1)], ident_f32[:])
-            live["c_ps", q], live["o_ps", q] = c_ps, o_ps
 
         def cell_out(q):
             c, half = divmod(q, HALVES)
             feats = slice(P * half, P * (half + 1))
             if half == 0:
-                live["c_out", c] = work.tile([P, CHUNK_TILES, HID], F32, name="c_out", tag="c_out")
-                live["h_out", c] = work.tile([P, CHUNK_TILES, HID], F32, name="h_out", tag="h_out")
-            nc.vector.tensor_copy(out=live["c_out", c][:, :, feats], in_=live["c_ps", q][:])
-            tanh_c = work.tile([P, CHUNK_TILES, P], F32, tag="tanh_c")
-            nc.scalar.activation(out=tanh_c[:], in_=live["c_out", c][:, :, feats], func=ACT.Tanh)
-            live["tanh_c", q] = tanh_c
+                live["c_out", c] = work.tile([P, tiles_in[c], HID], F32, name="c_out", tag="c_out")
+                live["h_out", c] = work.tile([P, tiles_in[c], HID], F32, name="h_out", tag="h_out")
+            c_ps = psum.tile([P, WIDEST // P, P], F32, tag="turn", bufs=3)
+            for t in range(tiles_in[c]):
+                nodes = slice(P * t, P * (t + 1))
+                nc.tensor.matmul(
+                    out=c_ps[:, t, :], lhsT=live["iu", q][:, nodes], rhs=ident_f32[:], is_transpose=True, start=True, stop=False
+                )
+                nc.tensor.matmul(
+                    out=c_ps[:, t, :], lhsT=live["c_red", q][:, nodes], rhs=ident_f32[:], is_transpose=True, start=False, stop=True
+                )
+            nc.vector.tensor_copy(out=live["c_out", c][:, :, feats], in_=c_ps[:, 0 : tiles_in[c], :])
             if half == HALVES - 1:
                 nc.sync.dma_start(out=c_out_view[:, tiles_of[c], :], in_=live["c_out", c][:])
+
+        def tanh_cell(q):
+            c, half = divmod(q, HALVES)
+            feats = slice(P * half, P * (half + 1))
+            tanh_c = work.tile([P, tiles_in[c], P], F32, tag="tanh_c")
+            nc.scalar.activation(out=tanh_c[:], in_=live["c_out", c][:, :, feats], func=ACT.Tanh)
+            live["tanh_c", q] = tanh_c
 
         def hidden_out(q):
             c, half = divmod(q, HALVES)
             feats = slice(P * half, P * (half + 1))
+            o_ps = psum.tile([P, WIDEST // P, P], F32, tag="turn", bufs=3)
+            for t in range(tiles_in[c]):
+                nc.tensor.transpose(o_ps[:, t, :], live["o_sb", q][:, P * t : P * (t + 1)], ident_f32[:])
             nc.vector.tensor_tensor(
-                out=live["h_out", c][:, :, feats], in0=live["tanh_c", q][:], in1=live["o_ps", q][:], op=ALU.mult
+                out=live["h_out", c][:, :, feats], in0=live["tanh_c", q][:], in1=o_ps[:, 0 : tiles_in[c], :], op=ALU.mult
             )
             if half == HALVES - 1:
                 nc.sync.dma_start(out=h_out_view[:, tiles_of[c], :], in_=live["h_out", c][:])
 
-        turn_h(0)
-        turn_h(1)
-        group_h(0)
-        group_h(1)
-        quantise_h(0)
-        bias_ps = psum.tile([P, CHILDREN, CHUNK], BF16, tag="cm_ps")
-        nc.tensor.transpose(bias_ps[:, 0, 0:P], bias_rows[:], ident_bf16[:])
-        nc.vector.tensor_copy(out=bias_sb[:], in_=bias_ps[:, 0, 0:GATE_TILES])
-        quantise_h(1)
+        def prepare_h(g):
+            turn_h(g)
+            group_h(g)
+
+        for g in range(CHUNK_PAIRS[0]):
+            prepare_h(g)
+        for g in range(CHUNK_PAIRS[0]):
+            quantise_h(g)
+        turn_bias()
 
         for q in range(UNITS + 3):
+            ahead = [g for g in range(CHUNK_PAIRS[0] + q + min(q, 1), CHUNK_PAIRS[0] + q + 2) if g < PAIRS]
             if q < UNITS:
                 gates(q)
                 turn_cm(q)
+                products(q)
+            if 0 <= q - 3 < UNITS:
+                tanh_cell(q - 3)
+            if 0 <= q - 2 < UNITS:
+                cell_out(q - 2)
+            for g in ahead:
+                prepare_h(g)
             if 0 <= q - 3 < UNITS:
                 hidden_out(q - 3)
-            if q == 1:
-                quantise_h(2)
-            if 1 <= q and q + 2 < PAIRS:
-                quantise_h(q + 2)
-            if q < UNITS:
-                products(q)
-            if 0 <= q - 2 < UNITS:
-                turn_back(q - 2)
-                cell_out(q - 2)
-            if 0 <= q - 1 < UNITS:
-                cell(q - 1)
-            if q == 0:
-                turn_h(2)
-                group_h(2)
-            if q + 3 < PAIRS:
-                turn_h(q + 3)
-                group_h(q + 3)
+            for g in ahead:
+                quantise_h(g)

@@ -70,7 +70,7 @@ def tile_treelstmcell_kernel(
             w_scales[w] = keep.tile([P, cols_of[w]], U8, align_bytes=64, name="w_scales_" + w)
         bias_rows = keep.tile([P, P], BF16)
         bias_sb = keep.tile([P, GATE_TILES], F32)
-        h_sb = [keep.tile([P, tiles_in[c], D], BF16, name="h_sb%d" % c) for c in range(CHUNKS)]
+        h_sb = [keep.tile([P, 2, D], BF16, name="h_sb%d" % g) for g in range(PAIRS)]
         cm_sb = [keep.tile([P, tiles_in[c], D], BF16, name="cm_sb%d" % c) for c in range(CHUNKS)]
         codes = [keep.tile([P, width[c]], U32, align_bytes=64, name="codes%d" % c) for c in range(CHUNKS)]
         scales = [keep.tile([P, width[c]], U8, align_bytes=64, name="scales%d" % c) for c in range(CHUNKS)]
@@ -78,9 +78,16 @@ def tile_treelstmcell_kernel(
         nc.vector.memset(bias_rows[:], 0.0)
         for w in ("f", "iou"):
             nc.vector.memset(w_scales[w][:].bitcast(I32), 0)
+        ident_f32 = keep.tile([P, P], F32)
+        make_identity(nc, ident_f32[:])
         nc.gpsimd.dma_start(out=bias_rows[0 : F_COLS // P, :], in_=U_f_b[0:F_COLS].rearrange("(m p) -> m p", p=P))
         nc.gpsimd.dma_start(out=bias_rows[F_COLS // P : GATE_TILES, :], in_=b_iou[0, :].rearrange("(m p) -> m p", p=P))
-        nc.scalar.dma_start(out=h_sb[0][:], in_=h_view[:, tiles_of[0], :])
+
+        def load_h(queue, g):
+            queue.dma_start(out=h_sb[g][:], in_=h_view[:, 2 * g : 2 * g + 2, :])
+
+        for g in range(CHUNK_PAIRS[0]):
+            load_h(nc.scalar, g)
 
         def load_weight(w, words, scale_rows):
             for quad in range(4):
@@ -93,15 +100,13 @@ def tile_treelstmcell_kernel(
         load_weight("f", U_f_w_words[0, :, 0 : 2 * F_COLS], U_f_w_scales[0, :, 0:F_COLS])
         load_weight("iou", U_iou_w_words[0, :, :], U_iou_w_scales[0, :, :])
         for c in range(CHUNKS):
-            if c + 1 < CHUNKS:
-                nc.sync.dma_start(out=h_sb[c + 1][:], in_=h_view[:, tiles_of[c + 1], :])
+            for g in range(CHUNK_PAIRS[0] + 2 * c, min(CHUNK_PAIRS[0] + 2 * (c + 1), PAIRS)):
+                load_h(nc.sync, g)
             nc.sync.dma_start(out=cm_sb[c][:], in_=cm_view[:, tiles_of[c], :])
 
         warm = keep.tile([P, 1], F32)
         nc.vector.memset(warm[:], 0.0)
         nc.scalar.activation(out=warm[:], in_=warm[:], func=ACT.Sigmoid)
-        ident_f32 = keep.tile([P, P], F32)
-        make_identity(nc, ident_f32[:])
         ident_bf16 = keep.tile([P, P], BF16)
         nc.vector.tensor_copy(out=ident_bf16[:], in_=ident_f32[:])
 
@@ -113,10 +118,9 @@ def tile_treelstmcell_kernel(
             nc.vector.tensor_copy(out=bias_sb[:], in_=bias_ps[:, 0, 0:GATE_TILES])
 
         def turn_h(g):
-            c = chunk_of_pair[g]
-            hT_ps = psum.tile([P, 2, 2, P], F32, tag="turn", bufs=3)
+            hT_ps = psum.tile([P, 2, 2, P], F32, tag="bank", bufs=7)
             for a in range(2):
-                words = h_sb[c][:, 2 * (g - first_pair[c]) + a, :].bitcast(F32)
+                words = h_sb[g][:, a, :].bitcast(F32)
                 for u in range(2):
                     nc.tensor.transpose(hT_ps[:, a, u, :], words[:, u : D // 2 : 2], ident_f32[:])
             live["hT_ps", g] = hT_ps
@@ -148,7 +152,7 @@ def tile_treelstmcell_kernel(
             live["cm_ps", q] = cm_ps
 
         def gate_pass(c, w, m):
-            gate_ps = psum.tile([P, WIDEST], F32, tag="gate_ps", bufs=4)
+            gate_ps = psum.tile([P, WIDEST], F32, tag="bank", bufs=7)
             nc.tensor.matmul_mx(
                 out=gate_ps[:, 0 : width[c]],
                 lhsT=w_words[w][:, 2 * P * m : 2 * P * (m + 1)].bitcast(FP4X4),
@@ -183,14 +187,15 @@ def tile_treelstmcell_kernel(
 
         def products(q):
             c = q // HALVES
+            helper = nc.vector if q == UNITS - 1 else nc.gpsimd
             prod = work.tile([P, CHILDREN, width[c]], F32, tag="prod")
             nc.vector.tensor_tensor(
                 out=prod[:], in0=live["f_sb", q][:], in1=live["cm_ps", q][:, :, 0 : width[c]], op=ALU.mult
             )
             c_red = work.tile([P, width[c]], F32, tag="c_red")
-            nc.gpsimd.tensor_tensor(out=c_red[:], in0=prod[:, 0, :], in1=prod[:, 1, :], op=ALU.add)
+            helper.tensor_tensor(out=c_red[:], in0=prod[:, 0, :], in1=prod[:, 1, :], op=ALU.add)
             iu = work.tile([P, width[c]], F32, tag="iu")
-            nc.gpsimd.tensor_tensor(out=iu[:], in0=live["i_sb", q][:], in1=live["u_sb", q][:], op=ALU.mult)
+            helper.tensor_tensor(out=iu[:], in0=live["i_sb", q][:], in1=live["u_sb", q][:], op=ALU.mult)
             live["c_red", q], live["iu", q] = c_red, iu
 
         def cell_out(q):
@@ -199,7 +204,7 @@ def tile_treelstmcell_kernel(
             if half == 0:
                 live["c_out", c] = work.tile([P, tiles_in[c], HID], F32, name="c_out", tag="c_out")
                 live["h_out", c] = work.tile([P, tiles_in[c], HID], F32, name="h_out", tag="h_out")
-            c_ps = psum.tile([P, WIDEST // P, P], F32, tag="turn", bufs=3)
+            c_ps = psum.tile([P, WIDEST // P, P], F32, tag="bank", bufs=7)
             for t in range(tiles_in[c]):
                 nodes = slice(P * t, P * (t + 1))
                 nc.tensor.matmul(
@@ -222,7 +227,7 @@ def tile_treelstmcell_kernel(
         def hidden_out(q):
             c, half = divmod(q, HALVES)
             feats = slice(P * half, P * (half + 1))
-            o_ps = psum.tile([P, WIDEST // P, P], F32, tag="turn", bufs=3)
+            o_ps = psum.tile([P, WIDEST // P, P], F32, tag="bank", bufs=7)
             for t in range(tiles_in[c]):
                 nc.tensor.transpose(o_ps[:, t, :], live["o_sb", q][:, P * t : P * (t + 1)], ident_f32[:])
             nc.vector.tensor_tensor(
@@ -242,7 +247,7 @@ def tile_treelstmcell_kernel(
         turn_bias()
 
         for q in range(UNITS + 3):
-            ahead = [g for g in range(CHUNK_PAIRS[0] + q + min(q, 1), CHUNK_PAIRS[0] + q + 2) if g < PAIRS]
+            ahead = [g for g in range(CHUNK_PAIRS[0] + 2 * q, CHUNK_PAIRS[0] + 2 * (q + 1)) if g < PAIRS]
             if q < UNITS:
                 gates(q)
                 turn_cm(q)

@@ -25,6 +25,8 @@ CHUNK_PAIRS = (2, 2, 2, 1, 1)
 CHUNKS = len(CHUNK_PAIRS)
 WIDEST = max(CHUNK_PAIRS) * PAIR
 HALVES = HID // P
+IDLE_BEFORE_H = 4
+IDLE_BEHIND_H = 2
 UNITS = CHUNKS * HALVES
 F_COLS = D
 IOU_COLS = 3 * HID
@@ -75,6 +77,8 @@ def tile_treelstmcell_kernel(
         codes = [keep.tile([P, width[c]], U32, align_bytes=64, name="codes%d" % c) for c in range(CHUNKS)]
         scales = [keep.tile([P, width[c]], U8, align_bytes=64, name="scales%d" % c) for c in range(CHUNKS)]
 
+        zeros = keep.tile([P, WIDEST], BF16)
+        nc.vector.memset(zeros[:], 0.0)
         nc.vector.memset(bias_rows[:], 0.0)
         for w in ("f", "iou"):
             nc.vector.memset(w_scales[w][:].bitcast(I32), 0)
@@ -88,6 +92,7 @@ def tile_treelstmcell_kernel(
 
         for g in range(CHUNK_PAIRS[0]):
             load_h(nc.scalar, g)
+        nc.scalar.dma_start(out=cm_sb[0][:], in_=cm_view[:, tiles_of[0], :])
 
         def load_weight(w, words, scale_rows):
             for quad in range(4):
@@ -102,7 +107,8 @@ def tile_treelstmcell_kernel(
         for c in range(CHUNKS):
             for g in range(CHUNK_PAIRS[0] + 2 * c, min(CHUNK_PAIRS[0] + 2 * (c + 1), PAIRS)):
                 load_h(nc.sync, g)
-            nc.sync.dma_start(out=cm_sb[c][:], in_=cm_view[:, tiles_of[c], :])
+            if c > 0:
+                nc.sync.dma_start(out=cm_sb[c][:], in_=cm_view[:, tiles_of[c], :])
 
         warm = keep.tile([P, 1], F32)
         nc.vector.memset(warm[:], 0.0)
@@ -240,8 +246,15 @@ def tile_treelstmcell_kernel(
             turn_h(g)
             group_h(g)
 
+        def idle_passes(n):
+            for k in range(n):
+                idle_ps = psum.tile([P, WIDEST], F32, tag="bank", bufs=7)
+                nc.tensor.matmul(out=idle_ps[:], lhsT=zeros[:, 0:P], rhs=zeros[:], start=True, stop=True)
+
+        idle_passes(IDLE_BEFORE_H)
         for g in range(CHUNK_PAIRS[0]):
             prepare_h(g)
+        idle_passes(IDLE_BEHIND_H)
         for g in range(CHUNK_PAIRS[0]):
             quantise_h(g)
         turn_bias()

@@ -198,11 +198,14 @@ def tile_treelstmcell_kernel(
             nc.vector.tensor_tensor(
                 out=prod[:], in0=live["f_sb", q][:], in1=live["cm_ps", q][:, :, 0 : width[c]], op=ALU.mult
             )
-            c_red = work.tile([P, width[c]], F32, tag="c_red")
-            helper.tensor_tensor(out=c_red[:], in0=prod[:, 0, :], in1=prod[:, 1, :], op=ALU.add)
             iu = work.tile([P, width[c]], F32, tag="iu")
+            if q < UNITS - 1:
+                c_red = work.tile([P, width[c]], F32, tag="c_red")
+                helper.tensor_tensor(out=c_red[:], in0=prod[:, 0, :], in1=prod[:, 1, :], op=ALU.add)
+                live["terms", q] = [iu[:], c_red[:]]
+            else:
+                live["terms", q] = [prod[:, 0, :], prod[:, 1, :], iu[:]]
             helper.tensor_tensor(out=iu[:], in0=live["i_sb", q][:], in1=live["u_sb", q][:], op=ALU.mult)
-            live["c_red", q], live["iu", q] = c_red, iu
 
         def cell_out(q):
             c, half = divmod(q, HALVES)
@@ -211,23 +214,29 @@ def tile_treelstmcell_kernel(
                 live["c_out", c] = work.tile([P, tiles_in[c], HID], F32, name="c_out", tag="c_out")
                 live["h_out", c] = work.tile([P, tiles_in[c], HID], F32, name="h_out", tag="h_out")
             c_ps = psum.tile([P, WIDEST // P, P], F32, tag="bank", bufs=7)
+            terms = live["terms", q]
             for t in range(tiles_in[c]):
                 nodes = slice(P * t, P * (t + 1))
-                nc.tensor.matmul(
-                    out=c_ps[:, t, :], lhsT=live["iu", q][:, nodes], rhs=ident_f32[:], is_transpose=True, start=True, stop=False
-                )
-                nc.tensor.matmul(
-                    out=c_ps[:, t, :], lhsT=live["c_red", q][:, nodes], rhs=ident_f32[:], is_transpose=True, start=False, stop=True
-                )
-            nc.vector.tensor_copy(out=live["c_out", c][:, :, feats], in_=c_ps[:, 0 : tiles_in[c], :])
-            if half == HALVES - 1:
-                nc.sync.dma_start(out=c_out_view[:, tiles_of[c], :], in_=live["c_out", c][:])
+                for s, term in enumerate(terms):
+                    nc.tensor.matmul(
+                        out=c_ps[:, t, :], lhsT=term[:, nodes], rhs=ident_f32[:], is_transpose=True, start=s == 0, stop=s == len(terms) - 1
+                    )
+            if q < UNITS - 1:
+                nc.vector.tensor_copy(out=live["c_out", c][:, :, feats], in_=c_ps[:, 0 : tiles_in[c], :])
+                if half == HALVES - 1:
+                    nc.sync.dma_start(out=c_out_view[:, tiles_of[c], :], in_=live["c_out", c][:])
+            live["c_ps", q] = c_ps
 
         def tanh_cell(q):
             c, half = divmod(q, HALVES)
             feats = slice(P * half, P * (half + 1))
             tanh_c = work.tile([P, tiles_in[c], P], F32, tag="tanh_c")
-            nc.scalar.activation(out=tanh_c[:], in_=live["c_out", c][:, :, feats], func=ACT.Tanh)
+            if q < UNITS - 1:
+                nc.scalar.activation(out=tanh_c[:], in_=live["c_out", c][:, :, feats], func=ACT.Tanh)
+            else:
+                nc.scalar.activation(out=tanh_c[:], in_=live["c_ps", q][:, 0 : tiles_in[c], :], func=ACT.Tanh)
+                nc.scalar.copy(out=live["c_out", c][:, :, feats], in_=live["c_ps", q][:, 0 : tiles_in[c], :])
+                nc.sync.dma_start(out=c_out_view[:, tiles_of[c], :], in_=live["c_out", c][:])
             live["tanh_c", q] = tanh_c
 
         def hidden_out(q):

@@ -193,13 +193,13 @@ def tile_treelstmcell_kernel(
 
         def products(q):
             c = q // HALVES
-            helper = nc.vector if q == UNITS - 1 else nc.gpsimd
+            helper = nc.vector if q >= UNITS - 2 else nc.gpsimd
             prod = work.tile([P, CHILDREN, width[c]], F32, tag="prod")
             nc.vector.tensor_tensor(
                 out=prod[:], in0=live["f_sb", q][:], in1=live["cm_ps", q][:, :, 0 : width[c]], op=ALU.mult
             )
             iu = work.tile([P, width[c]], F32, tag="iu")
-            if q < UNITS - 1:
+            if q < UNITS - 2:
                 c_red = work.tile([P, width[c]], F32, tag="c_red")
                 helper.tensor_tensor(out=c_red[:], in0=prod[:, 0, :], in1=prod[:, 1, :], op=ALU.add)
                 live["terms", q] = [iu[:], c_red[:]]

from contextlib import ExitStack

import concourse.mybir as mybir
from concourse.masks import make_identity

F32 = mybir.dt.float32
BF16 = mybir.dt.bfloat16
I32 = mybir.dt.int32
U32 = mybir.dt.uint32
U8 = mybir.dt.uint8
FP8X4 = mybir.dt.float8_e4m3fn_x4
FP4X4 = mybir.dt.float4_e2m1fn_x4
ACT = mybir.ActivationFunctionType
ALU = mybir.AluOpType

P = 128
NODES = 2048
CHILDREN = 2
HID = 256
D = CHILDREN * HID
TILES = NODES // P
PAIRS = TILES // 2
PAIR = 2 * P
CHUNK_PAIRS = (2, 2, 2, 1, 1)
CHUNKS = len(CHUNK_PAIRS)
WIDEST = max(CHUNK_PAIRS) * PAIR
HALVES = HID // P
IDLE_BEFORE_H = 4
IDLE_BEHIND_H = 2
UNITS = CHUNKS * HALVES
F_COLS = D
IOU_COLS = 3 * HID
W_COLS = F_COLS + IOU_COLS
GATE_TILES = W_COLS // P

FLOPS = 2 * NODES * D * W_COLS
BYTES = (
    2 * NODES * D * 2
    + P * W_COLS * 2 + 16 * W_COLS
    + W_COLS * 2
    + 2 * NODES * HID * 4
)


def tile_treelstmcell_kernel(
    tc, h_mail, c_mail, U_f_w_words, U_f_w_scales, U_f_b, U_iou_w_words, U_iou_w_scales, b_iou, out_0, out_1
):
    nc = tc.nc
    h_view = h_mail.rearrange("(p t) k j -> p t (k j)", t=TILES)
    cm_view = c_mail.rearrange("(p t) k j -> p t (k j)", t=TILES)
    h_out_view = out_0.rearrange("(p t) j -> p t j", t=TILES)
    c_out_view = out_1.rearrange("(p t) j -> p t j", t=TILES)

    first_pair = [sum(CHUNK_PAIRS[:c]) for c in range(CHUNKS)]
    chunk_of_pair = [c for c in range(CHUNKS) for g in range(CHUNK_PAIRS[c])]
    tiles_in = [2 * CHUNK_PAIRS[c] for c in range(CHUNKS)]
    width = [PAIR * CHUNK_PAIRS[c] for c in range(CHUNKS)]
    tiles_of = [slice(2 * first_pair[c], 2 * first_pair[c] + tiles_in[c]) for c in range(CHUNKS)]

    with ExitStack() as ctx:
        ctx.enter_context(tc.manual_schedule())
        keep = ctx.enter_context(tc.tile_pool(name="keep", bufs=1))
        work = ctx.enter_context(tc.tile_pool(name="work", bufs=5))
        psum = ctx.enter_context(tc.psum_pool(name="psum", bufs=1))

        cols_of = {"f": F_COLS, "iou": IOU_COLS}
        bias_col = {"f": 0, "iou": F_COLS // P}
        w_words = {}
        w_scales = {}
        for w in ("f", "iou"):
            w_words[w] = keep.tile([P, 2 * cols_of[w]], U8, align_bytes=64, name="w_words_" + w)
            w_scales[w] = keep.tile([P, cols_of[w]], U8, align_bytes=64, name="w_scales_" + w)
        bias_rows = keep.tile([P, P], BF16)
        bias_sb = keep.tile([P, GATE_TILES], F32)
        h_sb = [keep.tile([P, 2, D], BF16, name="h_sb%d" % g) for g in range(PAIRS)]
        cm_sb = [keep.tile([P, tiles_in[c], D], BF16, name="cm_sb%d" % c) for c in range(CHUNKS)]
        codes = [keep.tile([P, width[c]], U32, align_bytes=64, name="codes%d" % c) for c in range(CHUNKS)]
        scales = [keep.tile([P, width[c]], U8, align_bytes=64, name="scales%d" % c) for c in range(CHUNKS)]

        zeros = keep.tile([P, WIDEST], BF16)
        nc.vector.memset(zeros[:], 0.0)
        nc.vector.memset(bias_rows[:], 0.0)
        for w in ("f", "iou"):
            nc.vector.memset(w_scales[w][:].bitcast(I32), 0)
        ident_f32 = keep.tile([P, P], F32)
        make_identity(nc, ident_f32[:])
        nc.gpsimd.dma_start(out=bias_rows[0 : F_COLS // P, :], in_=U_f_b[0:F_COLS].rearrange("(m p) -> m p", p=P))
        nc.gpsimd.dma_start(out=bias_rows[F_COLS // P : GATE_TILES, :], in_=b_iou[0, :].rearrange("(m p) -> m p", p=P))

        def load_h(queue, g):
            queue.dma_start(out=h_sb[g][:], in_=h_view[:, 2 * g : 2 * g + 2, :])

        for g in range(CHUNK_PAIRS[0]):
            load_h(nc.scalar, g)
        nc.scalar.dma_start(out=cm_sb[0][:], in_=cm_view[:, tiles_of[0], :])

        def load_weight(w, words, scale_rows):
            for quad in range(4):
                nc.sync.dma_start(
                    out=w_scales[w][32 * quad : 32 * quad + 4, :].bitcast(I32),
                    in_=scale_rows[4 * quad : 4 * quad + 4, :].bitcast(I32),
                )
            nc.sync.dma_start(out=w_words[w][:].bitcast(I32), in_=words.bitcast(I32))

        load_weight("f", U_f_w_words[0, :, 0 : 2 * F_COLS], U_f_w_scales[0, :, 0:F_COLS])
        load_weight("iou", U_iou_w_words[0, :, :], U_iou_w_scales[0, :, :])
        for c in range(CHUNKS):
            for g in range(CHUNK_PAIRS[0] + 2 * c, min(CHUNK_PAIRS[0] + 2 * (c + 1), PAIRS)):
                load_h(nc.sync, g)
            if c > 0:
                nc.sync.dma_start(out=cm_sb[c][:], in_=cm_view[:, tiles_of[c], :])

        warm = keep.tile([P, 1], F32)
        nc.vector.memset(warm[:], 0.0)
        nc.scalar.activation(out=warm[:], in_=warm[:], func=ACT.Sigmoid)
        ident_bf16 = keep.tile([P, P], BF16)
        nc.vector.tensor_copy(out=ident_bf16[:], in_=ident_f32[:])

        live = {}

        def turn_bias():
            bias_ps = psum.tile([P, CHILDREN, WIDEST], BF16, tag="cm_ps")
            nc.tensor.transpose(bias_ps[:, 0, 0:P], bias_rows[:], ident_bf16[:])
            nc.vector.tensor_copy(out=bias_sb[:], in_=bias_ps[:, 0, 0:GATE_TILES])

        def turn_h(g):
            hT_ps = psum.tile([P, 2, 2, P], F32, tag="bank", bufs=7)
            for a in range(2):
                words = h_sb[g][:, a, :].bitcast(F32)
                for u in range(2):
                    nc.tensor.transpose(hT_ps[:, a, u, :], words[:, u : D // 2 : 2], ident_f32[:])
            live["hT_ps", g] = hT_ps

        def group_h(g):
            grouped = work.tile([P, PAIR, 4], BF16, align_bytes=64, tag="grouped")
            flat = grouped[:].rearrange("p n t -> p (n t)")
            nc.vector.tensor_copy(
                out=flat.bitcast(F32).rearrange("p (a n u) -> p a n u", a=2, u=2),
                in_=live["hT_ps", g][:].rearrange("p a u n -> p a n u"),
            )
            live["flat", g] = flat

        def quantise_h(g):
            c = chunk_of_pair[g]
            cols = slice(PAIR * (g - first_pair[c]), PAIR * (g - first_pair[c] + 1))
            nc.vector.quantize_mx(out=codes[c][:, cols].bitcast(FP8X4), scales=scales[c][:, cols], in_=live["flat", g])

        def turn_cm(q):
            c, half = divmod(q, HALVES)
            cm_ps = psum.tile([P, CHILDREN, WIDEST], BF16, tag="cm_ps")
            for k in range(CHILDREN):
                for t in range(tiles_in[c]):
                    nc.tensor.transpose(
                        cm_ps[:, k, P * t : P * (t + 1)],
                        cm_sb[c][:, t, HID * k + P * half : HID * k + P * (half + 1)],
                        ident_bf16[:],
                    )
            live["cm_ps", q] = cm_ps

        def gate_pass(c, w, m):
            gate_ps = psum.tile([P, WIDEST], F32, tag="bank", bufs=7)
            nc.tensor.matmul_mx(
                out=gate_ps[:, 0 : width[c]],
                lhsT=w_words[w][:, 2 * P * m : 2 * P * (m + 1)].bitcast(FP4X4),
                lhsT_scale=w_scales[w][:, P * m : P * (m + 1)],
                rhs=codes[c][:].bitcast(FP8X4),
                rhs_scale=scales[c][:],
                start=True,
                stop=True,
            )
            return gate_ps

        def gates(q):
            c, half = divmod(q, HALVES)
            f_sb = work.tile([P, CHILDREN, width[c]], F32, tag="f_sb")
            i_sb = work.tile([P, width[c]], F32, tag="i_sb")
            o_sb = work.tile([P, width[c]], F32, tag="o_sb")
            u_sb = work.tile([P, width[c]], F32, tag="u_sb")
            plan = [
                ("f", 0 * HALVES + half, ACT.Sigmoid, f_sb[:, 0, :]),
                ("f", 1 * HALVES + half, ACT.Sigmoid, f_sb[:, 1, :]),
                ("iou", 0 * HALVES + half, ACT.Sigmoid, i_sb[:]),
                ("iou", 2 * HALVES + half, ACT.Tanh, u_sb[:]),
                ("iou", 1 * HALVES + half, ACT.Sigmoid, o_sb[:]),
            ]
            banks = [gate_pass(c, w, m) for w, m, func, dest in plan]
            for (w, m, func, dest), gate_ps in zip(plan, banks):
                col = bias_col[w] + m
                nc.scalar.activation(
                    out=dest, in_=gate_ps[:, 0 : width[c]], func=func, bias=bias_sb[:, col : col + 1], scale=1.0
                )
            live["f_sb", q], live["i_sb", q], live["o_sb", q], live["u_sb", q] = f_sb, i_sb, o_sb, u_sb

        def products(q):
            c = q // HALVES
            helper = nc.vector if q >= UNITS - 2 else nc.gpsimd
            prod = work.tile([P, CHILDREN, width[c]], F32, tag="prod")
            nc.vector.tensor_tensor(
                out=prod[:], in0=live["f_sb", q][:], in1=live["cm_ps", q][:, :, 0 : width[c]], op=ALU.mult
            )
            iu = work.tile([P, width[c]], F32, tag="iu")
            if q < UNITS - 2:
                c_red = work.tile([P, width[c]], F32, tag="c_red")
                helper.tensor_tensor(out=c_red[:], in0=prod[:, 0, :], in1=prod[:, 1, :], op=ALU.add)
                live["terms", q] = [iu[:], c_red[:]]
            else:
                live["terms", q] = [prod[:, 0, :], prod[:, 1, :], iu[:]]
            helper.tensor_tensor(out=iu[:], in0=live["i_sb", q][:], in1=live["u_sb", q][:], op=ALU.mult)

        def cell_out(q):
            c, half = divmod(q, HALVES)
            feats = slice(P * half, P * (half + 1))
            if half == 0:
                live["c_out", c] = work.tile([P, tiles_in[c], HID], F32, name="c_out", tag="c_out")
                live["h_out", c] = work.tile([P, tiles_in[c], HID], F32, name="h_out", tag="h_out")
            c_ps = psum.tile([P, WIDEST // P, P], F32, tag="bank", bufs=7)
            terms = live["terms", q]
            for t in range(tiles_in[c]):
                nodes = slice(P * t, P * (t + 1))
                for s, term in enumerate(terms):
                    nc.tensor.matmul(
                        out=c_ps[:, t, :], lhsT=term[:, nodes], rhs=ident_f32[:], is_transpose=True, start=s == 0, stop=s == len(terms) - 1
                    )
            if q < UNITS - 1:
                nc.vector.tensor_copy(out=live["c_out", c][:, :, feats], in_=c_ps[:, 0 : tiles_in[c], :])
                if half == HALVES - 1:
                    nc.sync.dma_start(out=c_out_view[:, tiles_of[c], :], in_=live["c_out", c][:])
            live["c_ps", q] = c_ps

        def tanh_cell(q):
            c, half = divmod(q, HALVES)
            feats = slice(P * half, P * (half + 1))
            tanh_c = work.tile([P, tiles_in[c], P], F32, tag="tanh_c")
            if q < UNITS - 1:
                nc.scalar.activation(out=tanh_c[:], in_=live["c_out", c][:, :, feats], func=ACT.Tanh)
            else:
                nc.scalar.activation(out=tanh_c[:], in_=live["c_ps", q][:, 0 : tiles_in[c], :], func=ACT.Tanh)
                nc.scalar.copy(out=live["c_out", c][:, :, feats], in_=live["c_ps", q][:, 0 : tiles_in[c], :])
                nc.sync.dma_start(out=c_out_view[:, tiles_of[c], :], in_=live["c_out", c][:])
            live["tanh_c", q] = tanh_c

        def hidden_out(q):
            c, half = divmod(q, HALVES)
            feats = slice(P * half, P * (half + 1))
            o_ps = psum.tile([P, WIDEST // P, P], F32, tag="bank", bufs=7)
            for t in range(tiles_in[c]):
                nc.tensor.transpose(o_ps[:, t, :], live["o_sb", q][:, P * t : P * (t + 1)], ident_f32[:])
            nc.vector.tensor_tensor(
                out=live["h_out", c][:, :, feats], in0=live["tanh_c", q][:], in1=o_ps[:, 0 : tiles_in[c], :], op=ALU.mult
            )
            if half == HALVES - 1:
                nc.sync.dma_start(out=h_out_view[:, tiles_of[c], :], in_=live["h_out", c][:])

        def prepare_h(g):
            turn_h(g)
            group_h(g)

        def idle_passes(n):
            for k in range(n):
                idle_ps = psum.tile([P, WIDEST], F32, tag="bank", bufs=7)
                nc.tensor.matmul(out=idle_ps[:], lhsT=zeros[:, 0:P], rhs=zeros[:], start=True, stop=True)

        idle_passes(IDLE_BEFORE_H)
        for g in range(CHUNK_PAIRS[0]):
            prepare_h(g)
        idle_passes(IDLE_BEHIND_H)
        for g in range(CHUNK_PAIRS[0]):
            quantise_h(g)
        turn_bias()

        for q in range(UNITS + 3):
            ahead = [g for g in range(CHUNK_PAIRS[0] + 2 * q, CHUNK_PAIRS[0] + 2 * (q + 1)) if g < PAIRS]
            if q < UNITS:
                gates(q)
                turn_cm(q)
                products(q)
            if 0 <= q - 3 < UNITS:
                tanh_cell(q - 3)
            if 0 <= q - 2 < UNITS:
                cell_out(q - 2)
            for g in ahead:
                prepare_h(g)
            if 0 <= q - 3 < UNITS:
                hidden_out(q - 3)
            for g in ahead:
                quantise_h(g)
